import numpy as np
import ml_dtypes


def mxq(x, axis, fmt="e4m3"):
    dtype, down = {"e4m3": (ml_dtypes.float8_e4m3fn, 7), "e5m2": (ml_dtypes.float8_e5m2, 14)}[fmt]
    v = np.moveaxis(np.asarray(x, np.float32).astype(ml_dtypes.bfloat16).astype(np.float64), axis, -1)
    blocks = v.reshape(v.shape[:-1] + (-1, 32))
    amax = np.abs(blocks).max(-1, keepdims=True)
    byte = np.maximum(np.where(amax > 0, np.frexp(amax)[1] - 1 + 127, 0) - down, 1)
    scale = np.exp2(byte - 127.0)
    codes = (blocks / scale).astype(np.float32).astype(dtype).astype(np.float64)
    return np.moveaxis((codes * scale).reshape(v.shape), -1, axis)


WIDE = False


def mx_kscale(k):
    if not WIDE:
        return np.ones(k)
    levels = np.array([10, -10, 5, -5, 0])
    a = np.random.permutation(np.resize(levels, k // 512 * 4)).reshape(k // 512, 4)
    idx = np.arange(k)
    return np.exp2(a[idx // 512, idx % 128 // 32])


BF16 = ml_dtypes.bfloat16


def bf(x):
    return np.asarray(x, np.float32).astype(BF16)


def f64(x):
    return np.asarray(x).astype(np.float64)


L, B, D, D0 = 512, 8, 512, 768
EPS_BN = 1e-5
EPS_LN = 1e-5


def setup_inputs():
    n = np.random.standard_normal
    s = mx_kscale(D)
    r = n((B, L, D))
    return {"x": bf(n((L, B, D))), "res_a": bf(np.where(r > 0, r, 0.25 * r)),
            "ctx_v": bf(n((B, L, D)) * 0.25 * s), "W_v": bf(n((D, D)) * 2.0 / np.sqrt(D) / s[None, :]),
            "bn_v_g": bf(1.0 + 0.1 * n(D)), "bn_v_b": bf(0.2 * n(D)),
            "prelu_v": bf(0.25 + 0.05 * n(1)), "ln_g": bf(1.0 + 0.1 * n(D)), "ln_b": bf(0.2 * n(D))}


def reference(x, res_a, ctx_v, W_v, bn_v_g, bn_v_b, prelu_v, ln_g, ln_b):
    xq = np.swapaxes(f64(x), 0, 1)
    y = mxq(f64(ctx_v), 2, "e4m3") @ mxq(f64(W_v), 1, "e4m3").T
    mean = y.mean(axis=(0, 1))
    var = y.var(axis=(0, 1))
    z = (y - mean) / np.sqrt(var + EPS_BN) * f64(bn_v_g) + f64(bn_v_b)
    res_v = np.where(z > 0, z, f64(prelu_v) * z)
    out = np.swapaxes(xq + f64(res_a) + res_v, 0, 1)
    mu = out.mean(axis=-1, keepdims=True)
    v = out.var(axis=-1, keepdims=True)
    return (out - mu) / np.sqrt(v + EPS_LN) * f64(ln_g) + f64(ln_b)

@@ -1,0 +1,259 @@
+from contextlib import ExitStack
+
+import concourse.mybir as mybir
+from concourse.masks import make_identity
+
+F32 = mybir.dt.float32
+BF16 = mybir.dt.bfloat16
+U32 = mybir.dt.uint32
+U8 = mybir.dt.uint8
+FP8X4 = mybir.dt.float8_e4m3fn_x4
+ALU = mybir.AluOpType
+ACT = mybir.ActivationFunctionType
+
+L, B, D = 512, 8, 512
+P = 128
+EPS_BN = 1e-5
+EPS_LN = 1e-5
+TILES = 4
+BLOCKS = L * B // (TILES * P)
+CHUNKS = D // P
+WORDS = D // 2
+FLOPS = 2 * L * B * D * D
+
+
+def tile_coattention_pb_t_kernel(tc, x, res_a, ctx_v, W_v, bn_v_g, bn_v_b, prelu_v, ln_g, ln_b, out):
+    nc = tc.nc
+    with ExitStack() as stack:
+        stack.enter_context(tc.manual_schedule())
+        const = stack.enter_context(tc.tile_pool(name="const", bufs=1))
+        keep = stack.enter_context(tc.tile_pool(name="keep", bufs=1))
+        ctx_pool = stack.enter_context(tc.tile_pool(name="ctx", bufs=4))
+        stage = stack.enter_context(tc.tile_pool(name="stage", bufs=3))
+        branch = stack.enter_context(tc.tile_pool(name="branch", bufs=6))
+        small = stack.enter_context(tc.tile_pool(name="small", bufs=3))
+        gain_psum = stack.enter_context(tc.psum_pool(name="gain_psum", bufs=1))
+        y_psum = stack.enter_context(tc.psum_pool(name="y_psum", bufs=2))
+        turn_psum = stack.enter_context(tc.psum_pool(name="turn_psum", bufs=4))
+
+        def block_rows(blk):
+            group, half = divmod(blk, B // TILES)
+            return slice(group * P, (group + 1) * P), slice(half * TILES, (half + 1) * TILES)
+
+        eps_bn = const.tile([P, 1], F32, name="eps_bn")
+        nc.vector.memset(eps_bn[:], EPS_BN)
+        eps_ln = const.tile([P, 1], F32, name="eps_ln")
+        nc.vector.memset(eps_ln[:], EPS_LN)
+        warm = const.tile([P, 1], F32, name="warm")
+        nc.scalar.activation(out=warm[:], in_=eps_bn[:], func=ACT.Sqrt)
+
+        ones = const.tile([P, P], BF16, name="ones")
+        nc.vector.memset(ones[:], 1.0)
+        bn_rows = const.tile([P, P], BF16, name="bn_rows")
+        nc.vector.memset(bn_rows[:], 0.0)
+        ln_rows = const.tile([P, 2, D], BF16, name="ln_rows")
+        nc.vector.memset(ln_rows[:], 0.0)
+        slope_bf = const.tile([P, 1], BF16, name="slope_bf")
+        nc.scalar.dma_start(out=bn_rows[0:CHUNKS, :], in_=bn_v_g.rearrange("(c p) -> c p", p=P))
+        nc.scalar.dma_start(out=bn_rows[CHUNKS : 2 * CHUNKS, :], in_=bn_v_b.rearrange("(c p) -> c p", p=P))
+        nc.scalar.dma_start(out=ln_rows[0:1, 0, :], in_=ln_g.rearrange("(o d) -> o d", o=1))
+        nc.scalar.dma_start(out=ln_rows[0:1, 1, :], in_=ln_b.rearrange("(o d) -> o d", o=1))
+        nc.scalar.dma_start(out=slope_bf[:], in_=prelu_v.partition_broadcast(P))
+        ident_f32 = const.tile([P, P], F32, name="ident_f32")
+        make_identity(nc, ident_f32[:])
+        ident_bf = const.tile([P, P], BF16, name="ident_bf")
+        make_identity(nc, ident_bf[:])
+
+        w_sb = keep.tile([P, CHUNKS * D], BF16, name="w_sb")
+        nc.sync.dma_start(
+            out=w_sb[:].rearrange("p (c k) -> p c k", c=CHUNKS), in_=W_v.rearrange("(c p) k -> p c k", p=P)
+        )
+        ctx_sb = []
+        for blk in range(BLOCKS):
+            l_rows, b_rows = block_rows(blk)
+            ctx_t = ctx_pool.tile([P, TILES * D], BF16, name="ctx_t")
+            nc.sync.dma_start(
+                out=ctx_t[:].rearrange("p (b k) -> p b k", b=TILES),
+                in_=ctx_v[b_rows, l_rows, :].rearrange("b l k -> l b k"),
+            )
+            ctx_sb.append(ctx_t)
+        x_sb, res_sb = [], []
+        for blk in range(BLOCKS):
+            l_rows, b_rows = block_rows(blk)
+            x_t = keep.tile([P, TILES, D], BF16, name="x_t%d" % blk)
+            nc.sync.dma_start(out=x_t[:], in_=x[l_rows, b_rows, :])
+            res_t = keep.tile([P, TILES, D], BF16, name="res_t%d" % blk)
+            nc.sync.dma_start(out=res_t[:], in_=res_a[b_rows, l_rows, :].rearrange("b l d -> l b d"))
+            x_sb.append(x_t)
+            res_sb.append(res_t)
+
+        w_codes = keep.tile([P, D], U32, name="w_codes", align_bytes=64)
+        w_scales = keep.tile([P, D], U8, name="w_scales", align_bytes=64)
+        ctx_codes = keep.tile([P, BLOCKS, TILES * P], U32, name="ctx_codes", align_bytes=64)
+        ctx_scales = keep.tile([P, BLOCKS, TILES * P], U8, name="ctx_scales", align_bytes=64)
+
+        def turn_k_onto_partitions(rows_sb):
+            words = rows_sb[:].bitcast(F32)
+            grouped = stage.tile([P, TILES * P * 4], BF16, name="grouped", align_bytes=64)
+            grouped_words = grouped[:].bitcast(F32).rearrange("p (c u) -> p c u", u=2)
+            for pair in range(TILES // 2):
+                turned = turn_psum.tile([P, 2, 2 * P], F32, name="turned", tag="turn")
+                for i in range(2):
+                    for u in range(2):
+                        first = (2 * pair + i) * WORDS + u * P
+                        nc.tensor.transpose(
+                            out=turned[:, u, i * P : (i + 1) * P], in_=words[:, first : first + P], identity=ident_f32[:]
+                        )
+                nc.scalar.copy(
+                    out=grouped_words[:, 2 * pair * P : 2 * (pair + 1) * P, :], in_=turned[:].rearrange("p u r -> p r u")
+                )
+            return grouped
+
+        def conv_pass(blk, chunk):
+            y_t = y_psum.tile([P, TILES * P], F32, name="y_t")
+            c_cols = slice(chunk * P, (chunk + 1) * P)
+            nc.tensor.matmul_mx(
+                out=y_t[:],
+                lhsT=w_codes[:, c_cols].bitcast(FP8X4),
+                lhsT_scale=w_scales[:, c_cols],
+                rhs=ctx_codes[:, blk, :].bitcast(FP8X4),
+                rhs_scale=ctx_scales[:, blk, :],
+                start=True,
+                stop=True,
+            )
+            return y_t
+
+        w_grouped = turn_k_onto_partitions(w_sb)
+        grouped_next = turn_k_onto_partitions(ctx_sb[0])
+        nc.vector.quantize_mx(out=w_codes[:].bitcast(FP8X4), scales=w_scales[:], in_=w_grouped[:])
+
+        bn_turned = turn_psum.tile([P, P], BF16, name="bn_turned", tag="turn")
+        nc.tensor.transpose(out=bn_turned[:], in_=bn_rows[:], identity=ident_bf[:])
+        bn_cols = const.tile([P, 2 * CHUNKS], F32, name="bn_cols")
+        nc.vector.tensor_copy(out=bn_cols[:], in_=bn_turned[:, 0 : 2 * CHUNKS])
+        ln_gain = gain_psum.tile([P, D], F32, name="ln_gain")
+        nc.tensor.matmul(out=ln_gain[:], lhsT=ones[:], rhs=ln_rows[:, 0, :], start=True, stop=True)
+        ln_bias = gain_psum.tile([P, D], F32, name="ln_bias")
+        nc.tensor.matmul(out=ln_bias[:], lhsT=ones[:], rhs=ln_rows[:, 1, :], start=True, stop=True)
+        slope = const.tile([P, 1], F32, name="slope")
+        nc.vector.tensor_copy(out=slope[:], in_=slope_bf[:])
+        one_minus_slope = const.tile([P, 1], F32, name="one_minus_slope")
+        nc.vector.tensor_scalar(
+            out=one_minus_slope[:], in0=slope[:], scalar1=-1.0, scalar2=1.0, op0=ALU.mult, op1=ALU.add
+        )
+
+        stats = keep.tile([P, CHUNKS, BLOCKS, 6], F32, name="stats")
+        for blk in range(BLOCKS):
+            grouped = grouped_next
+            if blk + 1 < BLOCKS:
+                grouped_next = turn_k_onto_partitions(ctx_sb[blk + 1])
+            nc.vector.quantize_mx(
+                out=ctx_codes[:, blk, :].bitcast(FP8X4), scales=ctx_scales[:, blk, :], in_=grouped[:]
+            )
+            for chunk in range(CHUNKS):
+                y_t = conv_pass(blk, chunk)
+                nc.vector.bn_stats(out=stats[:, chunk, blk, :], in_=y_t[:])
+
+        sums = []
+        for blk in range(BLOCKS):
+            sum_t = keep.tile([P, TILES, D], F32, name="sum_t%d" % blk)
+            for j in range(TILES):
+                nc.gpsimd.tensor_tensor(out=sum_t[:, j, :], in0=x_sb[blk][:, j, :], in1=res_sb[blk][:, j, :], op=ALU.add)
+            sums.append(sum_t)
+
+        mean_var = const.tile([P, CHUNKS, 2], F32, name="mean_var")
+        for chunk in range(CHUNKS):
+            nc.vector.bn_aggr(out=mean_var[:, chunk, :], in_=stats[:, chunk, :, :].rearrange("p b s -> p (b s)"))
+        bn_std = const.tile([P, CHUNKS], F32, name="bn_std")
+        nc.scalar.activation(out=bn_std[:], in_=mean_var[:, :, 1], func=ACT.Sqrt, bias=eps_bn[:], scale=1.0)
+        bn_rstd = const.tile([P, CHUNKS], F32, name="bn_rstd")
+        nc.vector.reciprocal(out=bn_rstd[:], in_=bn_std[:])
+        bn_scale = const.tile([P, CHUNKS], F32, name="bn_scale")
+        nc.vector.tensor_mul(out=bn_scale[:], in0=bn_cols[:, 0:CHUNKS], in1=bn_rstd[:])
+        bn_shift = const.tile([P, CHUNKS], F32, name="bn_shift")
+        nc.vector.tensor_mul(out=bn_shift[:], in0=mean_var[:, :, 0], in1=bn_scale[:])
+        nc.vector.tensor_sub(out=bn_shift[:], in0=bn_cols[:, CHUNKS : 2 * CHUNKS], in1=bn_shift[:])
+        slope_scale = const.tile([P, CHUNKS], F32, name="slope_scale")
+        nc.vector.tensor_scalar_mul(out=slope_scale[:], in0=bn_scale[:], scalar1=slope[:])
+        slope_shift = const.tile([P, CHUNKS], F32, name="slope_shift")
+        nc.vector.tensor_scalar_mul(out=slope_shift[:], in0=bn_shift[:], scalar1=slope[:])
+
+        lines, relus, turned_back, neg_means = {}, {}, {}, {}
+
+        def affine(blk):
+            for chunk in range(CHUNKS):
+                col = slice(chunk, chunk + 1)
+                y_t = conv_pass(blk, chunk)
+                line = branch.tile([P, TILES * P], F32, name="line")
+                nc.scalar.activation(
+                    out=line[:], in_=y_t[:], func=ACT.Identity, bias=slope_shift[:, col], scale=slope_scale[:, col]
+                )
+                relu = branch.tile([P, TILES * P], F32, name="relu")
+                nc.scalar.activation(out=relu[:], in_=y_t[:], func=ACT.Relu, bias=bn_shift[:, col], scale=bn_scale[:, col])
+                lines[(blk, chunk)] = line
+                relus[(blk, chunk)] = relu
+
+        def combine(blk, chunk):
+            if chunk == 0:
+                turned_back[blk] = [turn_psum.tile([P, D], F32, name="back%d" % j, tag="turn") for j in range(TILES)]
+            res_v = stage.tile([P, TILES * P], F32, name="res_v")
+            nc.vector.scalar_tensor_tensor(
+                out=res_v[:], in0=relus[(blk, chunk)][:], scalar=one_minus_slope[:], in1=lines[(blk, chunk)][:],
+                op0=ALU.mult, op1=ALU.add,
+            )
+            for j in range(TILES):
+                nc.tensor.transpose(
+                    out=turned_back[blk][j][:, chunk * P : (chunk + 1) * P], in_=res_v[:, j * P : (j + 1) * P],
+                    identity=ident_f32[:],
+                )
+
+        def add_streams(blk):
+            row_sum = small.tile([P, TILES], F32, name="row_sum")
+            for j in range(TILES):
+                nc.vector.scalar_tensor_tensor(
+                    out=sums[blk][:, j, :], in0=turned_back[blk][j][:], scalar=1.0, in1=sums[blk][:, j, :],
+                    op0=ALU.mult, op1=ALU.add, accum_out=row_sum[:, j : j + 1],
+                )
+            neg_mean = small.tile([P, TILES], F32, name="neg_mean")
+            nc.vector.tensor_scalar_mul(out=neg_mean[:], in0=row_sum[:], scalar1=-1.0 / D)
+            neg_means[blk] = neg_mean
+
+        def deviation(blk):
+            square_sum = small.tile([P, TILES], F32, name="square_sum")
+            for j in range(TILES):
+                unread = branch.tile([P, D], BF16, name="unread")
+                nc.scalar.activation(
+                    out=unread[:], in_=sums[blk][:, j, :], func=ACT.Square, bias=neg_means[blk][:, j : j + 1], scale=1.0,
+                    accum_out=square_sum[:, j : j + 1],
+                )
+            row_std = small.tile([P, TILES], F32, name="row_std")
+            nc.scalar.activation(out=row_std[:], in_=square_sum[:], func=ACT.Sqrt, bias=eps_ln[:], scale=1.0 / D)
+            return row_std
+
+        affine(0)
+        for chunk in range(CHUNKS):
+            combine(0, chunk)
+        affine(1)
+        add_streams(0)
+        for blk in range(BLOCKS):
+            l_rows, b_rows = block_rows(blk)
+            row_std = deviation(blk)
+            if blk + 2 < BLOCKS:
+                affine(blk + 2)
+            for j in range(TILES):
+                if blk + 1 < BLOCKS:
+                    combine(blk + 1, j)
+                nc.vector.scalar_tensor_tensor(
+                    out=sums[blk][:, j, :], in0=sums[blk][:, j, :], scalar=neg_means[blk][:, j : j + 1], in1=ln_gain[:],
+                    op0=ALU.add, op1=ALU.mult,
+                )
+            row_rstd = small.tile([P, TILES], F32, name="row_rstd")
+            nc.vector.reciprocal(out=row_rstd[:], in_=row_std[:])
+            for j in range(TILES):
+                nc.vector.scalar_tensor_tensor(
+                    out=sums[blk][:, j, :], in0=sums[blk][:, j, :], scalar=row_rstd[:, j : j + 1], in1=ln_bias[:],
+                    op0=ALU.mult, op1=ALU.add,
+                )
+            nc.sync.dma_start(out=out[l_rows, b_rows, :], in_=sums[blk][:])
+            if blk + 1 < BLOCKS:
+                add_streams(blk + 1)

@@ -19,6 +19,7 @@ TILES = 4
 BLOCKS = L * B // (TILES * P)
 CHUNKS = D // P
 WORDS = D // 2
+HELPED = 2
 FLOPS = 2 * L * B * D * D
 
 
@@ -30,7 +31,8 @@ def tile_coattention_pb_t_kernel(tc, x, res_a, ctx_v, W_v, bn_v_g, bn_v_b, prelu
         keep = stack.enter_context(tc.tile_pool(name="keep", bufs=1))
         ctx_pool = stack.enter_context(tc.tile_pool(name="ctx", bufs=4))
         stage = stack.enter_context(tc.tile_pool(name="stage", bufs=3))
-        branch = stack.enter_context(tc.tile_pool(name="branch", bufs=6))
+        branch = stack.enter_context(tc.tile_pool(name="branch", bufs=2 * CHUNKS))
+        scrap = stack.enter_context(tc.tile_pool(name="scrap", bufs=4))
         small = stack.enter_context(tc.tile_pool(name="small", bufs=3))
         gain_psum = stack.enter_context(tc.psum_pool(name="gain_psum", bufs=1))
         y_psum = stack.enter_context(tc.psum_pool(name="y_psum", bufs=2))
@@ -141,6 +143,13 @@ def tile_coattention_pb_t_kernel(tc, x, res_a, ctx_v, W_v, bn_v_g, bn_v_b, prelu
         nc.vector.tensor_scalar(
             out=one_minus_slope[:], in0=slope[:], scalar1=-1.0, scalar2=1.0, op0=ALU.mult, op1=ALU.add
         )
+        flip = const.tile([P, 1], F32, name="flip")
+        nc.vector.tensor_scalar(out=flip[:], in0=one_minus_slope[:], scalar1=0.0, scalar2=2.0, op0=ALU.is_ge, op1=ALU.mult)
+        nc.vector.tensor_scalar_add(out=flip[:], in0=flip[:], scalar1=-1.0)
+        line_factor = const.tile([P, 1], F32, name="line_factor")
+        nc.vector.tensor_mul(out=line_factor[:], in0=slope[:], in1=flip[:])
+        relu_factor = const.tile([P, 1], F32, name="relu_factor")
+        nc.vector.tensor_mul(out=relu_factor[:], in0=one_minus_slope[:], in1=flip[:])
 
         stats = keep.tile([P, CHUNKS, BLOCKS, 6], F32, name="stats")
         for blk in range(BLOCKS):
@@ -173,87 +182,104 @@ def tile_coattention_pb_t_kernel(tc, x, res_a, ctx_v, W_v, bn_v_g, bn_v_b, prelu
         bn_shift = const.tile([P, CHUNKS], F32, name="bn_shift")
         nc.vector.tensor_mul(out=bn_shift[:], in0=mean_var[:, :, 0], in1=bn_scale[:])
         nc.vector.tensor_sub(out=bn_shift[:], in0=bn_cols[:, CHUNKS : 2 * CHUNKS], in1=bn_shift[:])
-        slope_scale = const.tile([P, CHUNKS], F32, name="slope_scale")
-        nc.vector.tensor_scalar_mul(out=slope_scale[:], in0=bn_scale[:], scalar1=slope[:])
-        slope_shift = const.tile([P, CHUNKS], F32, name="slope_shift")
-        nc.vector.tensor_scalar_mul(out=slope_shift[:], in0=bn_shift[:], scalar1=slope[:])
+        line_scale = const.tile([P, CHUNKS], F32, name="line_scale")
+        nc.vector.tensor_scalar_mul(out=line_scale[:], in0=bn_scale[:], scalar1=line_factor[:])
+        line_shift = const.tile([P, CHUNKS], F32, name="line_shift")
+        nc.vector.tensor_scalar_mul(out=line_shift[:], in0=bn_shift[:], scalar1=line_factor[:])
+        relu_scale = const.tile([P, CHUNKS], F32, name="relu_scale")
+        nc.vector.tensor_scalar_mul(out=relu_scale[:], in0=bn_scale[:], scalar1=relu_factor[:])
+        relu_shift = const.tile([P, CHUNKS], F32, name="relu_shift")
+        nc.vector.tensor_scalar_mul(out=relu_shift[:], in0=bn_shift[:], scalar1=relu_factor[:])
+        neg_relu_shift = const.tile([P, CHUNKS], F32, name="neg_relu_shift")
+        nc.vector.tensor_scalar_mul(out=neg_relu_shift[:], in0=relu_shift[:], scalar1=-1.0)
+        both_shifts = const.tile([P, CHUNKS], F32, name="both_shifts")
+        nc.vector.tensor_add(out=both_shifts[:], in0=line_shift[:], in1=relu_shift[:])
 
-        lines, relus, turned_back, neg_means = {}, {}, {}, {}
+        lines, relus, turned_back, row_sums, neg_means, row_stds = {}, {}, {}, {}, {}, {}
 
-        def affine(blk):
-            for chunk in range(CHUNKS):
-                col = slice(chunk, chunk + 1)
-                y_t = conv_pass(blk, chunk)
-                line = branch.tile([P, TILES * P], F32, name="line")
+        def affine(blk, chunk):
+            col = slice(chunk, chunk + 1)
+            y_t = conv_pass(blk, chunk)
+            line = branch.tile([P, TILES * P], F32, name="line")
+            relu = branch.tile([P, TILES * P], F32, name="relu")
+            if blk < HELPED and chunk % 2 == 1:
+                nc.vector.tensor_scalar(
+                    out=line[:], in0=y_t[:], scalar1=line_scale[:, col], scalar2=both_shifts[:, col],
+                    op0=ALU.mult, op1=ALU.add,
+                )
+                nc.vector.tensor_scalar(
+                    out=relu[:], in0=y_t[:], scalar1=relu_scale[:, col], scalar2=neg_relu_shift[:, col],
+                    op0=ALU.mult, op1=ALU.max,
+                )
+            else:
                 nc.scalar.activation(
-                    out=line[:], in_=y_t[:], func=ACT.Identity, bias=slope_shift[:, col], scale=slope_scale[:, col]
+                    out=line[:], in_=y_t[:], func=ACT.Identity, bias=line_shift[:, col], scale=line_scale[:, col]
                 )
-                relu = branch.tile([P, TILES * P], F32, name="relu")
-                nc.scalar.activation(out=relu[:], in_=y_t[:], func=ACT.Relu, bias=bn_shift[:, col], scale=bn_scale[:, col])
-                lines[(blk, chunk)] = line
-                relus[(blk, chunk)] = relu
+                nc.scalar.activation(
+                    out=relu[:], in_=y_t[:], func=ACT.Relu, bias=relu_shift[:, col], scale=relu_scale[:, col]
+                )
+            lines[(blk, chunk)] = line
+            relus[(blk, chunk)] = relu
 
-        def combine(blk, chunk):
-            if chunk == 0:
-                turned_back[blk] = [turn_psum.tile([P, D], F32, name="back%d" % j, tag="turn") for j in range(TILES)]
-            res_v = stage.tile([P, TILES * P], F32, name="res_v")
+        def turn_back(blk, j):
+            back = turn_psum.tile([P, D], F32, name="back", tag="turn")
+            for chunk in range(CHUNKS):
+                for term, first in ((lines[(blk, chunk)], True), (relus[(blk, chunk)], False)):
+                    nc.tensor.matmul(
+                        out=back[:, chunk * P : (chunk + 1) * P], lhsT=term[:, j * P : (j + 1) * P],
+                        rhs=ident_f32[:], is_transpose=True, start=first, stop=not first,
+                    )
+            turned_back[(blk, j)] = back
+
+        def add_streams(blk, j):
+            if j == 0:
+                row_sums[blk] = small.tile([P, TILES], F32, name="row_sum")
             nc.vector.scalar_tensor_tensor(
-                out=res_v[:], in0=relus[(blk, chunk)][:], scalar=one_minus_slope[:], in1=lines[(blk, chunk)][:],
-                op0=ALU.mult, op1=ALU.add,
+                out=sums[blk][:, j, :], in0=turned_back[(blk, j)][:], scalar=flip[:], in1=sums[blk][:, j, :],
+                op0=ALU.mult, op1=ALU.add, accum_out=row_sums[blk][:, j : j + 1],
             )
-            for j in range(TILES):
-                nc.tensor.transpose(
-                    out=turned_back[blk][j][:, chunk * P : (chunk + 1) * P], in_=res_v[:, j * P : (j + 1) * P],
-                    identity=ident_f32[:],
-                )
-
-        def add_streams(blk):
-            row_sum = small.tile([P, TILES], F32, name="row_sum")
-            for j in range(TILES):
-                nc.vector.scalar_tensor_tensor(
-                    out=sums[blk][:, j, :], in0=turned_back[blk][j][:], scalar=1.0, in1=sums[blk][:, j, :],
-                    op0=ALU.mult, op1=ALU.add, accum_out=row_sum[:, j : j + 1],
-                )
-            neg_mean = small.tile([P, TILES], F32, name="neg_mean")
-            nc.vector.tensor_scalar_mul(out=neg_mean[:], in0=row_sum[:], scalar1=-1.0 / D)
-            neg_means[blk] = neg_mean
 
         def deviation(blk):
+            neg_mean = small.tile([P, TILES], F32, name="neg_mean")
+            nc.vector.tensor_scalar_mul(out=neg_mean[:], in0=row_sums[blk][:], scalar1=-1.0 / D)
             square_sum = small.tile([P, TILES], F32, name="square_sum")
             for j in range(TILES):
-                unread = branch.tile([P, D], BF16, name="unread")
+                unread = scrap.tile([P, D], BF16, name="unread")
                 nc.scalar.activation(
-                    out=unread[:], in_=sums[blk][:, j, :], func=ACT.Square, bias=neg_means[blk][:, j : j + 1], scale=1.0,
+                    out=unread[:], in_=sums[blk][:, j, :], func=ACT.Square, bias=neg_mean[:, j : j + 1], scale=1.0,
                     accum_out=square_sum[:, j : j + 1],
                 )
             row_std = small.tile([P, TILES], F32, name="row_std")
             nc.scalar.activation(out=row_std[:], in_=square_sum[:], func=ACT.Sqrt, bias=eps_ln[:], scale=1.0 / D)
-            return row_std
+            neg_means[blk] = neg_mean
+            row_stds[blk] = row_std
 
-        affine(0)
-        for chunk in range(CHUNKS):
-            combine(0, chunk)
-        affine(1)
-        add_streams(0)
-        for blk in range(BLOCKS):
+        def normalise(blk):
             l_rows, b_rows = block_rows(blk)
-            row_std = deviation(blk)
-            if blk + 2 < BLOCKS:
-                affine(blk + 2)
+            first_b = (blk % (B // TILES)) * TILES
+            row_rstd = small.tile([P, TILES], F32, name="row_rstd")
+            nc.vector.reciprocal(out=row_rstd[:], in_=row_stds[blk][:])
             for j in range(TILES):
-                if blk + 1 < BLOCKS:
-                    combine(blk + 1, j)
                 nc.vector.scalar_tensor_tensor(
                     out=sums[blk][:, j, :], in0=sums[blk][:, j, :], scalar=neg_means[blk][:, j : j + 1], in1=ln_gain[:],
                     op0=ALU.add, op1=ALU.mult,
                 )
-            row_rstd = small.tile([P, TILES], F32, name="row_rstd")
-            nc.vector.reciprocal(out=row_rstd[:], in_=row_std[:])
             for j in range(TILES):
                 nc.vector.scalar_tensor_tensor(
                     out=sums[blk][:, j, :], in0=sums[blk][:, j, :], scalar=row_rstd[:, j : j + 1], in1=ln_bias[:],
                     op0=ALU.mult, op1=ALU.add,
                 )
-            nc.sync.dma_start(out=out[l_rows, b_rows, :], in_=sums[blk][:])
-            if blk + 1 < BLOCKS:
-                add_streams(blk + 1)
+                nc.sync.dma_start(out=out[l_rows, first_b + j : first_b + j + 1, :], in_=sums[blk][:, j : j + 1, :])
+
+        for step in range(-3, BLOCKS):
+            for j in range(TILES):
+                if 0 <= step + 3 < BLOCKS:
+                    affine(step + 3, j)
+                if 0 <= step + 1 < BLOCKS:
+                    add_streams(step + 1, j)
+                if 0 <= step + 2 < BLOCKS:
+                    turn_back(step + 2, j)
+            if 0 <= step + 1 < BLOCKS:
+                deviation(step + 1)
+            if 0 <= step:
+                normalise(step)

@@ -35,7 +35,7 @@ def tile_coattention_pb_t_kernel(tc, x, res_a, ctx_v, W_v, bn_v_g, bn_v_b, prelu
         scrap = stack.enter_context(tc.tile_pool(name="scrap", bufs=4))
         small = stack.enter_context(tc.tile_pool(name="small", bufs=3))
         gain_psum = stack.enter_context(tc.psum_pool(name="gain_psum", bufs=1))
-        y_psum = stack.enter_context(tc.psum_pool(name="y_psum", bufs=2))
+        y_psum = stack.enter_context(tc.psum_pool(name="y_psum", bufs=3))
         turn_psum = stack.enter_context(tc.psum_pool(name="turn_psum", bufs=4))
 
         def block_rows(blk):
@@ -133,10 +133,11 @@ def tile_coattention_pb_t_kernel(tc, x, res_a, ctx_v, W_v, bn_v_g, bn_v_b, prelu
         nc.tensor.transpose(out=bn_turned[:], in_=bn_rows[:], identity=ident_bf[:])
         bn_cols = const.tile([P, 2 * CHUNKS], F32, name="bn_cols")
         nc.vector.tensor_copy(out=bn_cols[:], in_=bn_turned[:, 0 : 2 * CHUNKS])
-        ln_gain = gain_psum.tile([P, D], F32, name="ln_gain")
-        nc.tensor.matmul(out=ln_gain[:], lhsT=ones[:], rhs=ln_rows[:, 0, :], start=True, stop=True)
-        ln_bias = gain_psum.tile([P, D], F32, name="ln_bias")
-        nc.tensor.matmul(out=ln_bias[:], lhsT=ones[:], rhs=ln_rows[:, 1, :], start=True, stop=True)
+        ln_both = gain_psum.tile([P, 2, D], BF16, name="ln_both")
+        nc.tensor.matmul(out=ln_both[:, 0, :], lhsT=ones[:], rhs=ln_rows[:, 0, :], start=True, stop=True)
+        nc.tensor.matmul(out=ln_both[:, 1, :], lhsT=ones[:], rhs=ln_rows[:, 1, :], start=True, stop=True)
+        ln_gain = ln_both[:, 0, :]
+        ln_bias = ln_both[:, 1, :]
         slope = const.tile([P, 1], F32, name="slope")
         nc.vector.tensor_copy(out=slope[:], in_=slope_bf[:])
         one_minus_slope = const.tile([P, 1], F32, name="one_minus_slope")
@@ -261,25 +262,28 @@ def tile_coattention_pb_t_kernel(tc, x, res_a, ctx_v, W_v, bn_v_g, bn_v_b, prelu
             nc.vector.reciprocal(out=row_rstd[:], in_=row_stds[blk][:])
             for j in range(TILES):
                 nc.vector.scalar_tensor_tensor(
-                    out=sums[blk][:, j, :], in0=sums[blk][:, j, :], scalar=neg_means[blk][:, j : j + 1], in1=ln_gain[:],
+                    out=sums[blk][:, j, :], in0=sums[blk][:, j, :], scalar=neg_means[blk][:, j : j + 1], in1=ln_gain,
                     op0=ALU.add, op1=ALU.mult,
                 )
             for j in range(TILES):
                 nc.vector.scalar_tensor_tensor(
-                    out=sums[blk][:, j, :], in0=sums[blk][:, j, :], scalar=row_rstd[:, j : j + 1], in1=ln_bias[:],
+                    out=sums[blk][:, j, :], in0=sums[blk][:, j, :], scalar=row_rstd[:, j : j + 1], in1=ln_bias,
                     op0=ALU.mult, op1=ALU.add,
                 )
                 nc.sync.dma_start(out=out[l_rows, first_b + j : first_b + j + 1, :], in_=sums[blk][:, j : j + 1, :])
 
         for step in range(-3, BLOCKS):
-            for j in range(TILES):
+            for half in range(2):
+                pair = (2 * half, 2 * half + 1)
                 if 0 <= step + 3 < BLOCKS:
-                    affine(step + 3, j)
-                if 0 <= step + 1 < BLOCKS:
-                    add_streams(step + 1, j)
+                    for chunk in pair:
+                        affine(step + 3, chunk)
+                if half == 0 and 0 <= step + 1 < BLOCKS:
+                    for j in range(TILES):
+                        add_streams(step + 1, j)
+                    deviation(step + 1)
                 if 0 <= step + 2 < BLOCKS:
-                    turn_back(step + 2, j)
-            if 0 <= step + 1 < BLOCKS:
-                deviation(step + 1)
+                    for j in pair:
+                        turn_back(step + 2, j)
             if 0 <= step:
                 normalise(step)

@@ -203,7 +203,7 @@ def tile_coattention_pb_t_kernel(tc, x, res_a, ctx_v, W_v, bn_v_g, bn_v_b, prelu
             y_t = conv_pass(blk, chunk)
             line = branch.tile([P, TILES * P], F32, name="line")
             relu = branch.tile([P, TILES * P], F32, name="relu")
-            if blk < HELPED and chunk % 2 == 1:
+            if chunk == CHUNKS - 1 or (blk < HELPED and chunk == 1):
                 nc.vector.tensor_scalar(
                     out=line[:], in0=y_t[:], scalar1=line_scale[:, col], scalar2=both_shifts[:, col],
                     op0=ALU.mult, op1=ALU.add,

@@ -47,7 +47,7 @@ def tile_coattention_pb_t_kernel(tc, x, res_a, ctx_v, W_v, bn_v_g, bn_v_b, prelu
         eps_ln = const.tile([P, 1], F32, name="eps_ln")
         nc.vector.memset(eps_ln[:], EPS_LN)
         warm = const.tile([P, 1], F32, name="warm")
-        nc.scalar.activation(out=warm[:], in_=eps_bn[:], func=ACT.Sqrt)
+        nc.scalar.activation(out=warm[:], in_=eps_bn[:], func=ACT.Abs_reciprocal_sqrt)
 
         ones = const.tile([P, P], BF16, name="ones")
         nc.vector.memset(ones[:], 1.0)
@@ -125,9 +125,29 @@ def tile_coattention_pb_t_kernel(tc, x, res_a, ctx_v, W_v, bn_v_g, bn_v_b, prelu
             )
             return y_t
 
+        grouped = {}
+        stats = keep.tile([P, CHUNKS, BLOCKS, 6], F32, name="stats")
+
+        def quantise(blk):
+            nc.vector.quantize_mx(
+                out=ctx_codes[:, blk, :].bitcast(FP8X4), scales=ctx_scales[:, blk, :], in_=grouped[blk][:]
+            )
+
+        def multiply(blk):
+            if blk + 2 < BLOCKS:
+                grouped[blk + 2] = turn_k_onto_partitions(ctx_sb[blk + 2])
+            if blk + 1 < BLOCKS:
+                quantise(blk + 1)
+            for chunk in range(CHUNKS):
+                y_t = conv_pass(blk, chunk)
+                nc.vector.bn_stats(out=stats[:, chunk, blk, :], in_=y_t[:])
+
         w_grouped = turn_k_onto_partitions(w_sb)
-        grouped_next = turn_k_onto_partitions(ctx_sb[0])
+        grouped[0] = turn_k_onto_partitions(ctx_sb[0])
         nc.vector.quantize_mx(out=w_codes[:].bitcast(FP8X4), scales=w_scales[:], in_=w_grouped[:])
+        grouped[1] = turn_k_onto_partitions(ctx_sb[1])
+        quantise(0)
+        multiply(0)
 
         bn_turned = turn_psum.tile([P, P], BF16, name="bn_turned", tag="turn")
         nc.tensor.transpose(out=bn_turned[:], in_=bn_rows[:], identity=ident_bf[:])
@@ -152,17 +172,8 @@ def tile_coattention_pb_t_kernel(tc, x, res_a, ctx_v, W_v, bn_v_g, bn_v_b, prelu
         relu_factor = const.tile([P, 1], F32, name="relu_factor")
         nc.vector.tensor_mul(out=relu_factor[:], in0=one_minus_slope[:], in1=flip[:])
 
-        stats = keep.tile([P, CHUNKS, BLOCKS, 6], F32, name="stats")
-        for blk in range(BLOCKS):
-            grouped = grouped_next
-            if blk + 1 < BLOCKS:
-                grouped_next = turn_k_onto_partitions(ctx_sb[blk + 1])
-            nc.vector.quantize_mx(
-                out=ctx_codes[:, blk, :].bitcast(FP8X4), scales=ctx_scales[:, blk, :], in_=grouped[:]
-            )
-            for chunk in range(CHUNKS):
-                y_t = conv_pass(blk, chunk)
-                nc.vector.bn_stats(out=stats[:, chunk, blk, :], in_=y_t[:])
+        for blk in range(1, BLOCKS):
+            multiply(blk)
 
         sums = []
         for blk in range(BLOCKS):
@@ -174,10 +185,10 @@ def tile_coattention_pb_t_kernel(tc, x, res_a, ctx_v, W_v, bn_v_g, bn_v_b, prelu
         mean_var = const.tile([P, CHUNKS, 2], F32, name="mean_var")
         for chunk in range(CHUNKS):
             nc.vector.bn_aggr(out=mean_var[:, chunk, :], in_=stats[:, chunk, :, :].rearrange("p b s -> p (b s)"))
-        bn_std = const.tile([P, CHUNKS], F32, name="bn_std")
-        nc.scalar.activation(out=bn_std[:], in_=mean_var[:, :, 1], func=ACT.Sqrt, bias=eps_bn[:], scale=1.0)
         bn_rstd = const.tile([P, CHUNKS], F32, name="bn_rstd")
-        nc.vector.reciprocal(out=bn_rstd[:], in_=bn_std[:])
+        nc.scalar.activation(
+            out=bn_rstd[:], in_=mean_var[:, :, 1], func=ACT.Abs_reciprocal_sqrt, bias=eps_bn[:], scale=1.0
+        )
         bn_scale = const.tile([P, CHUNKS], F32, name="bn_scale")
         nc.vector.tensor_mul(out=bn_scale[:], in0=bn_cols[:, 0:CHUNKS], in1=bn_rstd[:])
         bn_shift = const.tile([P, CHUNKS], F32, name="bn_shift")
@@ -196,14 +207,14 @@ def tile_coattention_pb_t_kernel(tc, x, res_a, ctx_v, W_v, bn_v_g, bn_v_b, prelu
         both_shifts = const.tile([P, CHUNKS], F32, name="both_shifts")
         nc.vector.tensor_add(out=both_shifts[:], in0=line_shift[:], in1=relu_shift[:])
 
-        lines, relus, turned_back, row_sums, neg_means, row_stds = {}, {}, {}, {}, {}, {}
+        lines, relus, turned_back, row_sums, neg_means, row_rstds = {}, {}, {}, {}, {}, {}
 
         def affine(blk, chunk):
             col = slice(chunk, chunk + 1)
             y_t = conv_pass(blk, chunk)
             line = branch.tile([P, TILES * P], F32, name="line")
             relu = branch.tile([P, TILES * P], F32, name="relu")
-            if chunk == CHUNKS - 1 or (blk < HELPED and chunk == 1):
+            if blk < HELPED and chunk % 2 == 1:
                 nc.vector.tensor_scalar(
                     out=line[:], in0=y_t[:], scalar1=line_scale[:, col], scalar2=both_shifts[:, col],
                     op0=ALU.mult, op1=ALU.add,
@@ -242,7 +253,7 @@ def tile_coattention_pb_t_kernel(tc, x, res_a, ctx_v, W_v, bn_v_g, bn_v_b, prelu
 
         def deviation(blk):
             neg_mean = small.tile([P, TILES], F32, name="neg_mean")
-            nc.vector.tensor_scalar_mul(out=neg_mean[:], in0=row_sums[blk][:], scalar1=-1.0 / D)
+            nc.scalar.mul(out=neg_mean[:], in_=row_sums[blk][:], mul=-1.0 / D)
             square_sum = small.tile([P, TILES], F32, name="square_sum")
             for j in range(TILES):
                 unread = scrap.tile([P, D], BF16, name="unread")
@@ -250,16 +261,17 @@ def tile_coattention_pb_t_kernel(tc, x, res_a, ctx_v, W_v, bn_v_g, bn_v_b, prelu
                     out=unread[:], in_=sums[blk][:, j, :], func=ACT.Square, bias=neg_mean[:, j : j + 1], scale=1.0,
                     accum_out=square_sum[:, j : j + 1],
                 )
-            row_std = small.tile([P, TILES], F32, name="row_std")
-            nc.scalar.activation(out=row_std[:], in_=square_sum[:], func=ACT.Sqrt, bias=eps_ln[:], scale=1.0 / D)
+            row_rstd = small.tile([P, TILES], F32, name="row_rstd")
+            nc.scalar.activation(
+                out=row_rstd[:], in_=square_sum[:], func=ACT.Abs_reciprocal_sqrt, bias=eps_ln[:], scale=1.0 / D
+            )
             neg_means[blk] = neg_mean
-            row_stds[blk] = row_std
+            row_rstds[blk] = row_rstd
 
         def normalise(blk):
             l_rows, b_rows = block_rows(blk)
             first_b = (blk % (B // TILES)) * TILES
-            row_rstd = small.tile([P, TILES], F32, name="row_rstd")
-            nc.vector.reciprocal(out=row_rstd[:], in_=row_stds[blk][:])
+            row_rstd = row_rstds[blk]
             for j in range(TILES):
                 nc.vector.scalar_tensor_tensor(
                     out=sums[blk][:, j, :], in0=sums[blk][:, j, :], scalar=neg_means[blk][:, j : j + 1], in1=ln_gain,

@@ -31,12 +31,12 @@ def tile_coattention_pb_t_kernel(tc, x, res_a, ctx_v, W_v, bn_v_g, bn_v_b, prelu
         keep = stack.enter_context(tc.tile_pool(name="keep", bufs=1))
         ctx_pool = stack.enter_context(tc.tile_pool(name="ctx", bufs=4))
         stage = stack.enter_context(tc.tile_pool(name="stage", bufs=3))
+        streams = stack.enter_context(tc.tile_pool(name="streams", bufs=4))
         branch = stack.enter_context(tc.tile_pool(name="branch", bufs=2 * CHUNKS))
         scrap = stack.enter_context(tc.tile_pool(name="scrap", bufs=4))
         small = stack.enter_context(tc.tile_pool(name="small", bufs=3))
         gain_psum = stack.enter_context(tc.psum_pool(name="gain_psum", bufs=1))
-        y_psum = stack.enter_context(tc.psum_pool(name="y_psum", bufs=3))
-        turn_psum = stack.enter_context(tc.psum_pool(name="turn_psum", bufs=4))
+        banks = stack.enter_context(tc.psum_pool(name="banks", bufs=7))
 
         def block_rows(blk):
             group, half = divmod(blk, B // TILES)
@@ -82,74 +82,72 @@ def tile_coattention_pb_t_kernel(tc, x, res_a, ctx_v, W_v, bn_v_g, bn_v_b, prelu
         x_sb, res_sb = [], []
         for blk in range(BLOCKS):
             l_rows, b_rows = block_rows(blk)
-            x_t = keep.tile([P, TILES, D], BF16, name="x_t%d" % blk)
+            x_t = streams.tile([P, TILES, D], BF16, name="x_t")
             nc.sync.dma_start(out=x_t[:], in_=x[l_rows, b_rows, :])
-            res_t = keep.tile([P, TILES, D], BF16, name="res_t%d" % blk)
+            res_t = streams.tile([P, TILES, D], BF16, name="res_t")
             nc.sync.dma_start(out=res_t[:], in_=res_a[b_rows, l_rows, :].rearrange("b l d -> l b d"))
             x_sb.append(x_t)
             res_sb.append(res_t)
 
         w_codes = keep.tile([P, D], U32, name="w_codes", align_bytes=64)
         w_scales = keep.tile([P, D], U8, name="w_scales", align_bytes=64)
-        ctx_codes = keep.tile([P, BLOCKS, TILES * P], U32, name="ctx_codes", align_bytes=64)
-        ctx_scales = keep.tile([P, BLOCKS, TILES * P], U8, name="ctx_scales", align_bytes=64)
 
-        def turn_k_onto_partitions(rows_sb):
+        def turn_k_onto_partitions(rows_sb, share):
             words = rows_sb[:].bitcast(F32)
             grouped = stage.tile([P, TILES * P * 4], BF16, name="grouped", align_bytes=64)
             grouped_words = grouped[:].bitcast(F32).rearrange("p (c u) -> p c u", u=2)
             for pair in range(TILES // 2):
-                turned = turn_psum.tile([P, 2, 2 * P], F32, name="turned", tag="turn")
+                turned = banks.tile([P, 2, 2 * P], F32, name="turned", tag="bank")
                 for i in range(2):
                     for u in range(2):
                         first = (2 * pair + i) * WORDS + u * P
                         nc.tensor.transpose(
                             out=turned[:, u, i * P : (i + 1) * P], in_=words[:, first : first + P], identity=ident_f32[:]
                         )
-                nc.scalar.copy(
-                    out=grouped_words[:, 2 * pair * P : 2 * (pair + 1) * P, :], in_=turned[:].rearrange("p u r -> p r u")
-                )
+                copy = nc.vector.tensor_copy if share and pair == 1 else nc.scalar.copy
+                copy(out=grouped_words[:, 2 * pair * P : 2 * (pair + 1) * P, :], in_=turned[:].rearrange("p u r -> p r u"))
             return grouped
 
-        def conv_pass(blk, chunk):
-            y_t = y_psum.tile([P, TILES * P], F32, name="y_t")
-            c_cols = slice(chunk * P, (chunk + 1) * P)
-            nc.tensor.matmul_mx(
-                out=y_t[:],
-                lhsT=w_codes[:, c_cols].bitcast(FP8X4),
-                lhsT_scale=w_scales[:, c_cols],
-                rhs=ctx_codes[:, blk, :].bitcast(FP8X4),
-                rhs_scale=ctx_scales[:, blk, :],
-                start=True,
-                stop=True,
-            )
-            return y_t
-
-        grouped = {}
+        grouped, codes, y_sb = {}, {}, {}
         stats = keep.tile([P, CHUNKS, BLOCKS, 6], F32, name="stats")
 
         def quantise(blk):
-            nc.vector.quantize_mx(
-                out=ctx_codes[:, blk, :].bitcast(FP8X4), scales=ctx_scales[:, blk, :], in_=grouped[blk][:]
-            )
+            ctx_codes = stage.tile([P, TILES * P], U32, name="ctx_codes", align_bytes=64)
+            ctx_scales = stage.tile([P, TILES * P], U8, name="ctx_scales", align_bytes=64)
+            nc.vector.quantize_mx(out=ctx_codes[:].bitcast(FP8X4), scales=ctx_scales[:], in_=grouped[blk][:])
+            codes[blk] = (ctx_codes, ctx_scales)
 
         def multiply(blk):
             if blk + 2 < BLOCKS:
-                grouped[blk + 2] = turn_k_onto_partitions(ctx_sb[blk + 2])
+                grouped[blk + 2] = turn_k_onto_partitions(ctx_sb[blk + 2], blk % 2 == 1)
             if blk + 1 < BLOCKS:
                 quantise(blk + 1)
+            ctx_codes, ctx_scales = codes[blk]
             for chunk in range(CHUNKS):
-                y_t = conv_pass(blk, chunk)
+                c_cols = slice(chunk * P, (chunk + 1) * P)
+                y_bank = banks.tile([P, TILES * P], F32, name="y_bank", tag="bank")
+                nc.tensor.matmul_mx(
+                    out=y_bank[:],
+                    lhsT=w_codes[:, c_cols].bitcast(FP8X4),
+                    lhsT_scale=w_scales[:, c_cols],
+                    rhs=ctx_codes[:].bitcast(FP8X4),
+                    rhs_scale=ctx_scales[:],
+                    start=True,
+                    stop=True,
+                )
+                y_t = keep.tile([P, TILES * P], F32, name="y_t%d_%d" % (blk, chunk))
+                nc.scalar.copy(out=y_t[:], in_=y_bank[:])
                 nc.vector.bn_stats(out=stats[:, chunk, blk, :], in_=y_t[:])
+                y_sb[(blk, chunk)] = y_t
 
-        w_grouped = turn_k_onto_partitions(w_sb)
-        grouped[0] = turn_k_onto_partitions(ctx_sb[0])
+        w_grouped = turn_k_onto_partitions(w_sb, False)
+        grouped[0] = turn_k_onto_partitions(ctx_sb[0], False)
         nc.vector.quantize_mx(out=w_codes[:].bitcast(FP8X4), scales=w_scales[:], in_=w_grouped[:])
-        grouped[1] = turn_k_onto_partitions(ctx_sb[1])
+        grouped[1] = turn_k_onto_partitions(ctx_sb[1], False)
         quantise(0)
         multiply(0)
 
-        bn_turned = turn_psum.tile([P, P], BF16, name="bn_turned", tag="turn")
+        bn_turned = banks.tile([P, P], BF16, name="bn_turned", tag="bank")
         nc.tensor.transpose(out=bn_turned[:], in_=bn_rows[:], identity=ident_bf[:])
         bn_cols = const.tile([P, 2 * CHUNKS], F32, name="bn_cols")
         nc.vector.tensor_copy(out=bn_cols[:], in_=bn_turned[:, 0 : 2 * CHUNKS])
@@ -207,36 +205,34 @@ def tile_coattention_pb_t_kernel(tc, x, res_a, ctx_v, W_v, bn_v_g, bn_v_b, prelu
         both_shifts = const.tile([P, CHUNKS], F32, name="both_shifts")
         nc.vector.tensor_add(out=both_shifts[:], in0=line_shift[:], in1=relu_shift[:])
 
-        lines, relus, turned_back, row_sums, neg_means, row_rstds = {}, {}, {}, {}, {}, {}
+        relus, turned_back, row_sums, neg_means, row_rstds = {}, {}, {}, {}, {}
 
         def affine(blk, chunk):
             col = slice(chunk, chunk + 1)
-            y_t = conv_pass(blk, chunk)
-            line = branch.tile([P, TILES * P], F32, name="line")
+            y_t = y_sb[(blk, chunk)]
             relu = branch.tile([P, TILES * P], F32, name="relu")
             if blk < HELPED and chunk % 2 == 1:
-                nc.vector.tensor_scalar(
-                    out=line[:], in0=y_t[:], scalar1=line_scale[:, col], scalar2=both_shifts[:, col],
-                    op0=ALU.mult, op1=ALU.add,
-                )
                 nc.vector.tensor_scalar(
                     out=relu[:], in0=y_t[:], scalar1=relu_scale[:, col], scalar2=neg_relu_shift[:, col],
                     op0=ALU.mult, op1=ALU.max,
                 )
-            else:
-                nc.scalar.activation(
-                    out=line[:], in_=y_t[:], func=ACT.Identity, bias=line_shift[:, col], scale=line_scale[:, col]
+                nc.vector.tensor_scalar(
+                    out=y_t[:], in0=y_t[:], scalar1=line_scale[:, col], scalar2=both_shifts[:, col],
+                    op0=ALU.mult, op1=ALU.add,
                 )
+            else:
                 nc.scalar.activation(
                     out=relu[:], in_=y_t[:], func=ACT.Relu, bias=relu_shift[:, col], scale=relu_scale[:, col]
                 )
-            lines[(blk, chunk)] = line
+                nc.scalar.activation(
+                    out=y_t[:], in_=y_t[:], func=ACT.Identity, bias=line_shift[:, col], scale=line_scale[:, col]
+                )
             relus[(blk, chunk)] = relu
 
         def turn_back(blk, j):
-            back = turn_psum.tile([P, D], F32, name="back", tag="turn")
+            back = banks.tile([P, D], F32, name="back", tag="bank")
             for chunk in range(CHUNKS):
-                for term, first in ((lines[(blk, chunk)], True), (relus[(blk, chunk)], False)):
+                for term, first in ((y_sb[(blk, chunk)], True), (relus[(blk, chunk)], False)):
                     nc.tensor.matmul(
                         out=back[:, chunk * P : (chunk + 1) * P], lhsT=term[:, j * P : (j + 1) * P],
                         rhs=ident_f32[:], is_transpose=True, start=first, stop=not first,

@@ -29,14 +29,12 @@ def tile_coattention_pb_t_kernel(tc, x, res_a, ctx_v, W_v, bn_v_g, bn_v_b, prelu
         stack.enter_context(tc.manual_schedule())
         const = stack.enter_context(tc.tile_pool(name="const", bufs=1))
         keep = stack.enter_context(tc.tile_pool(name="keep", bufs=1))
-        ctx_pool = stack.enter_context(tc.tile_pool(name="ctx", bufs=4))
-        stage = stack.enter_context(tc.tile_pool(name="stage", bufs=3))
-        streams = stack.enter_context(tc.tile_pool(name="streams", bufs=4))
         branch = stack.enter_context(tc.tile_pool(name="branch", bufs=2 * CHUNKS))
         scrap = stack.enter_context(tc.tile_pool(name="scrap", bufs=4))
         small = stack.enter_context(tc.tile_pool(name="small", bufs=3))
         gain_psum = stack.enter_context(tc.psum_pool(name="gain_psum", bufs=1))
-        banks = stack.enter_context(tc.psum_pool(name="banks", bufs=7))
+        y_psum = stack.enter_context(tc.psum_pool(name="y_psum", bufs=3))
+        turn_psum = stack.enter_context(tc.psum_pool(name="turn_psum", bufs=4))
 
         def block_rows(blk):
             group, half = divmod(blk, B // TILES)
@@ -66,116 +64,123 @@ def tile_coattention_pb_t_kernel(tc, x, res_a, ctx_v, W_v, bn_v_g, bn_v_b, prelu
         ident_bf = const.tile([P, P], BF16, name="ident_bf")
         make_identity(nc, ident_bf[:])
 
-        w_sb = keep.tile([P, CHUNKS * D], BF16, name="w_sb")
-        nc.sync.dma_start(
-            out=w_sb[:].rearrange("p (c k) -> p c k", c=CHUNKS), in_=W_v.rearrange("(c p) k -> p c k", p=P)
-        )
-        ctx_sb = []
-        for blk in range(BLOCKS):
-            l_rows, b_rows = block_rows(blk)
-            ctx_t = ctx_pool.tile([P, TILES * D], BF16, name="ctx_t")
+        with tc.tile_pool(name="ctx", bufs=4) as ctx_pool, tc.tile_pool(name="stage", bufs=3) as stage:
+            w_sb = keep.tile([P, CHUNKS * D], BF16, name="w_sb")
             nc.sync.dma_start(
-                out=ctx_t[:].rearrange("p (b k) -> p b k", b=TILES),
-                in_=ctx_v[b_rows, l_rows, :].rearrange("b l k -> l b k"),
+                out=w_sb[:].rearrange("p (c k) -> p c k", c=CHUNKS), in_=W_v.rearrange("(c p) k -> p c k", p=P)
             )
-            ctx_sb.append(ctx_t)
-        x_sb, res_sb = [], []
-        for blk in range(BLOCKS):
-            l_rows, b_rows = block_rows(blk)
-            x_t = streams.tile([P, TILES, D], BF16, name="x_t")
-            nc.sync.dma_start(out=x_t[:], in_=x[l_rows, b_rows, :])
-            res_t = streams.tile([P, TILES, D], BF16, name="res_t")
-            nc.sync.dma_start(out=res_t[:], in_=res_a[b_rows, l_rows, :].rearrange("b l d -> l b d"))
-            x_sb.append(x_t)
-            res_sb.append(res_t)
+            ctx_sb = []
+            for blk in range(BLOCKS):
+                l_rows, b_rows = block_rows(blk)
+                ctx_t = ctx_pool.tile([P, TILES * D], BF16, name="ctx_t")
+                nc.sync.dma_start(
+                    out=ctx_t[:].rearrange("p (b k) -> p b k", b=TILES),
+                    in_=ctx_v[b_rows, l_rows, :].rearrange("b l k -> l b k"),
+                )
+                ctx_sb.append(ctx_t)
+            x_sb, res_sb = [], []
+            for blk in range(BLOCKS):
+                l_rows, b_rows = block_rows(blk)
+                x_t = keep.tile([P, TILES, D], BF16, name="x_t%d" % blk)
+                nc.sync.dma_start(out=x_t[:], in_=x[l_rows, b_rows, :])
+                res_t = keep.tile([P, TILES, D], BF16, name="res_t%d" % blk)
+                nc.sync.dma_start(out=res_t[:], in_=res_a[b_rows, l_rows, :].rearrange("b l d -> l b d"))
+                x_sb.append(x_t)
+                res_sb.append(res_t)
 
-        w_codes = keep.tile([P, D], U32, name="w_codes", align_bytes=64)
-        w_scales = keep.tile([P, D], U8, name="w_scales", align_bytes=64)
+            w_codes = keep.tile([P, D], U32, name="w_codes", align_bytes=64)
+            w_scales = keep.tile([P, D], U8, name="w_scales", align_bytes=64)
+            ctx_codes = keep.tile([P, BLOCKS, TILES * P], U32, name="ctx_codes", align_bytes=64)
+            ctx_scales = keep.tile([P, BLOCKS, TILES * P], U8, name="ctx_scales", align_bytes=64)
 
-        def turn_k_onto_partitions(rows_sb, share):
-            words = rows_sb[:].bitcast(F32)
-            grouped = stage.tile([P, TILES * P * 4], BF16, name="grouped", align_bytes=64)
-            grouped_words = grouped[:].bitcast(F32).rearrange("p (c u) -> p c u", u=2)
-            for pair in range(TILES // 2):
-                turned = banks.tile([P, 2, 2 * P], F32, name="turned", tag="bank")
-                for i in range(2):
-                    for u in range(2):
-                        first = (2 * pair + i) * WORDS + u * P
-                        nc.tensor.transpose(
-                            out=turned[:, u, i * P : (i + 1) * P], in_=words[:, first : first + P], identity=ident_f32[:]
-                        )
-                copy = nc.vector.tensor_copy if share and pair == 1 else nc.scalar.copy
-                copy(out=grouped_words[:, 2 * pair * P : 2 * (pair + 1) * P, :], in_=turned[:].rearrange("p u r -> p r u"))
-            return grouped
+            def turn_k_onto_partitions(rows_sb):
+                words = rows_sb[:].bitcast(F32)
+                grouped = stage.tile([P, TILES * P * 4], BF16, name="grouped", align_bytes=64)
+                grouped_words = grouped[:].bitcast(F32).rearrange("p (c u) -> p c u", u=2)
+                for pair in range(TILES // 2):
+                    turned = turn_psum.tile([P, 2, 2 * P], F32, name="turned", tag="turn")
+                    for i in range(2):
+                        for u in range(2):
+                            first = (2 * pair + i) * WORDS + u * P
+                            nc.tensor.transpose(
+                                out=turned[:, u, i * P : (i + 1) * P], in_=words[:, first : first + P], identity=ident_f32[:]
+                            )
+                    nc.scalar.copy(
+                        out=grouped_words[:, 2 * pair * P : 2 * (pair + 1) * P, :], in_=turned[:].rearrange("p u r -> p r u")
+                    )
+                return grouped
 
-        grouped, codes, y_sb = {}, {}, {}
-        stats = keep.tile([P, CHUNKS, BLOCKS, 6], F32, name="stats")
-
-        def quantise(blk):
-            ctx_codes = stage.tile([P, TILES * P], U32, name="ctx_codes", align_bytes=64)
-            ctx_scales = stage.tile([P, TILES * P], U8, name="ctx_scales", align_bytes=64)
-            nc.vector.quantize_mx(out=ctx_codes[:].bitcast(FP8X4), scales=ctx_scales[:], in_=grouped[blk][:])
-            codes[blk] = (ctx_codes, ctx_scales)
-
-        def multiply(blk):
-            if blk + 2 < BLOCKS:
-                grouped[blk + 2] = turn_k_onto_partitions(ctx_sb[blk + 2], blk % 2 == 1)
-            if blk + 1 < BLOCKS:
-                quantise(blk + 1)
-            ctx_codes, ctx_scales = codes[blk]
-            for chunk in range(CHUNKS):
+            def conv_pass(blk, chunk, bank_pool, bank_tag):
+                y_t = bank_pool.tile([P, TILES * P], F32, name="y_t", tag=bank_tag)
                 c_cols = slice(chunk * P, (chunk + 1) * P)
-                y_bank = banks.tile([P, TILES * P], F32, name="y_bank", tag="bank")
                 nc.tensor.matmul_mx(
-                    out=y_bank[:],
+                    out=y_t[:],
                     lhsT=w_codes[:, c_cols].bitcast(FP8X4),
                     lhsT_scale=w_scales[:, c_cols],
-                    rhs=ctx_codes[:].bitcast(FP8X4),
-                    rhs_scale=ctx_scales[:],
+                    rhs=ctx_codes[:, blk, :].bitcast(FP8X4),
+                    rhs_scale=ctx_scales[:, blk, :],
                     start=True,
                     stop=True,
                 )
-                y_t = keep.tile([P, TILES * P], F32, name="y_t%d_%d" % (blk, chunk))
-                nc.scalar.copy(out=y_t[:], in_=y_bank[:])
-                nc.vector.bn_stats(out=stats[:, chunk, blk, :], in_=y_t[:])
-                y_sb[(blk, chunk)] = y_t
+                return y_t
 
-        w_grouped = turn_k_onto_partitions(w_sb, False)
-        grouped[0] = turn_k_onto_partitions(ctx_sb[0], False)
-        nc.vector.quantize_mx(out=w_codes[:].bitcast(FP8X4), scales=w_scales[:], in_=w_grouped[:])
-        grouped[1] = turn_k_onto_partitions(ctx_sb[1], False)
-        quantise(0)
-        multiply(0)
+            grouped = {}
+            stats = keep.tile([P, CHUNKS, BLOCKS, 6], F32, name="stats")
 
-        bn_turned = banks.tile([P, P], BF16, name="bn_turned", tag="bank")
-        nc.tensor.transpose(out=bn_turned[:], in_=bn_rows[:], identity=ident_bf[:])
-        bn_cols = const.tile([P, 2 * CHUNKS], F32, name="bn_cols")
-        nc.vector.tensor_copy(out=bn_cols[:], in_=bn_turned[:, 0 : 2 * CHUNKS])
-        ln_both = gain_psum.tile([P, 2, D], BF16, name="ln_both")
-        nc.tensor.matmul(out=ln_both[:, 0, :], lhsT=ones[:], rhs=ln_rows[:, 0, :], start=True, stop=True)
-        nc.tensor.matmul(out=ln_both[:, 1, :], lhsT=ones[:], rhs=ln_rows[:, 1, :], start=True, stop=True)
-        ln_gain = ln_both[:, 0, :]
-        ln_bias = ln_both[:, 1, :]
-        slope = const.tile([P, 1], F32, name="slope")
-        nc.vector.tensor_copy(out=slope[:], in_=slope_bf[:])
-        one_minus_slope = const.tile([P, 1], F32, name="one_minus_slope")
-        nc.vector.tensor_scalar(
-            out=one_minus_slope[:], in0=slope[:], scalar1=-1.0, scalar2=1.0, op0=ALU.mult, op1=ALU.add
-        )
-        flip = const.tile([P, 1], F32, name="flip")
-        nc.vector.tensor_scalar(out=flip[:], in0=one_minus_slope[:], scalar1=0.0, scalar2=2.0, op0=ALU.is_ge, op1=ALU.mult)
-        nc.vector.tensor_scalar_add(out=flip[:], in0=flip[:], scalar1=-1.0)
-        line_factor = const.tile([P, 1], F32, name="line_factor")
-        nc.vector.tensor_mul(out=line_factor[:], in0=slope[:], in1=flip[:])
-        relu_factor = const.tile([P, 1], F32, name="relu_factor")
-        nc.vector.tensor_mul(out=relu_factor[:], in0=one_minus_slope[:], in1=flip[:])
+            def quantise(blk):
+                nc.vector.quantize_mx(
+                    out=ctx_codes[:, blk, :].bitcast(FP8X4), scales=ctx_scales[:, blk, :], in_=grouped[blk][:]
+                )
 
-        for blk in range(1, BLOCKS):
-            multiply(blk)
+            def multiply(blk):
+                if blk + 2 < BLOCKS:
+                    grouped[blk + 2] = turn_k_onto_partitions(ctx_sb[blk + 2])
+                if blk + 1 < BLOCKS:
+                    quantise(blk + 1)
+                for chunk in range(CHUNKS):
+                    if chunk % 2 == 0:
+                        y_t = conv_pass(blk, chunk, y_psum, "y")
+                    else:
+                        y_t = conv_pass(blk, chunk, turn_psum, "turn")
+                    nc.vector.bn_stats(out=stats[:, chunk, blk, :], in_=y_t[:])
 
+            w_grouped = turn_k_onto_partitions(w_sb)
+            grouped[0] = turn_k_onto_partitions(ctx_sb[0])
+            nc.vector.quantize_mx(out=w_codes[:].bitcast(FP8X4), scales=w_scales[:], in_=w_grouped[:])
+            grouped[1] = turn_k_onto_partitions(ctx_sb[1])
+            quantise(0)
+            multiply(0)
+
+            bn_turned = turn_psum.tile([P, P], BF16, name="bn_turned", tag="turn")
+            nc.tensor.transpose(out=bn_turned[:], in_=bn_rows[:], identity=ident_bf[:])
+            bn_cols = const.tile([P, 2 * CHUNKS], F32, name="bn_cols")
+            nc.vector.tensor_copy(out=bn_cols[:], in_=bn_turned[:, 0 : 2 * CHUNKS])
+            ln_both = gain_psum.tile([P, 2, D], BF16, name="ln_both")
+            nc.tensor.matmul(out=ln_both[:, 0, :], lhsT=ones[:], rhs=ln_rows[:, 0, :], start=True, stop=True)
+            nc.tensor.matmul(out=ln_both[:, 1, :], lhsT=ones[:], rhs=ln_rows[:, 1, :], start=True, stop=True)
+            ln_gain = ln_both[:, 0, :]
+            ln_bias = ln_both[:, 1, :]
+            slope = const.tile([P, 1], F32, name="slope")
+            nc.vector.tensor_copy(out=slope[:], in_=slope_bf[:])
+            one_minus_slope = const.tile([P, 1], F32, name="one_minus_slope")
+            nc.vector.tensor_scalar(
+                out=one_minus_slope[:], in0=slope[:], scalar1=-1.0, scalar2=1.0, op0=ALU.mult, op1=ALU.add
+            )
+            flip = const.tile([P, 1], F32, name="flip")
+            nc.vector.tensor_scalar(out=flip[:], in0=one_minus_slope[:], scalar1=0.0, scalar2=2.0, op0=ALU.is_ge, op1=ALU.mult)
+            nc.vector.tensor_scalar_add(out=flip[:], in0=flip[:], scalar1=-1.0)
+            line_factor = const.tile([P, 1], F32, name="line_factor")
+            nc.vector.tensor_mul(out=line_factor[:], in0=slope[:], in1=flip[:])
+            relu_factor = const.tile([P, 1], F32, name="relu_factor")
+            nc.vector.tensor_mul(out=relu_factor[:], in0=one_minus_slope[:], in1=flip[:])
+
+            for blk in range(1, BLOCKS):
+                multiply(blk)
+
+        sum_pool = stack.enter_context(tc.tile_pool(name="sums", bufs=1))
         sums = []
         for blk in range(BLOCKS):
-            sum_t = keep.tile([P, TILES, D], F32, name="sum_t%d" % blk)
+            sum_t = sum_pool.tile([P, TILES, D], F32, name="sum_t%d" % blk)
             for j in range(TILES):
                 nc.gpsimd.tensor_tensor(out=sum_t[:, j, :], in0=x_sb[blk][:, j, :], in1=res_sb[blk][:, j, :], op=ALU.add)
             sums.append(sum_t)
@@ -205,34 +210,36 @@ def tile_coattention_pb_t_kernel(tc, x, res_a, ctx_v, W_v, bn_v_g, bn_v_b, prelu
         both_shifts = const.tile([P, CHUNKS], F32, name="both_shifts")
         nc.vector.tensor_add(out=both_shifts[:], in0=line_shift[:], in1=relu_shift[:])
 
-        relus, turned_back, row_sums, neg_means, row_rstds = {}, {}, {}, {}, {}
+        lines, relus, turned_back, row_sums, neg_means, row_rstds = {}, {}, {}, {}, {}, {}
 
         def affine(blk, chunk):
             col = slice(chunk, chunk + 1)
-            y_t = y_sb[(blk, chunk)]
+            y_t = conv_pass(blk, chunk, y_psum, "y")
+            line = branch.tile([P, TILES * P], F32, name="line")
             relu = branch.tile([P, TILES * P], F32, name="relu")
             if blk < HELPED and chunk % 2 == 1:
+                nc.vector.tensor_scalar(
+                    out=line[:], in0=y_t[:], scalar1=line_scale[:, col], scalar2=both_shifts[:, col],
+                    op0=ALU.mult, op1=ALU.add,
+                )
                 nc.vector.tensor_scalar(
                     out=relu[:], in0=y_t[:], scalar1=relu_scale[:, col], scalar2=neg_relu_shift[:, col],
                     op0=ALU.mult, op1=ALU.max,
                 )
-                nc.vector.tensor_scalar(
-                    out=y_t[:], in0=y_t[:], scalar1=line_scale[:, col], scalar2=both_shifts[:, col],
-                    op0=ALU.mult, op1=ALU.add,
-                )
             else:
+                nc.scalar.activation(
+                    out=line[:], in_=y_t[:], func=ACT.Identity, bias=line_shift[:, col], scale=line_scale[:, col]
+                )
                 nc.scalar.activation(
                     out=relu[:], in_=y_t[:], func=ACT.Relu, bias=relu_shift[:, col], scale=relu_scale[:, col]
                 )
-                nc.scalar.activation(
-                    out=y_t[:], in_=y_t[:], func=ACT.Identity, bias=line_shift[:, col], scale=line_scale[:, col]
-                )
+            lines[(blk, chunk)] = line
             relus[(blk, chunk)] = relu
 
         def turn_back(blk, j):
-            back = banks.tile([P, D], F32, name="back", tag="bank")
+            back = turn_psum.tile([P, D], F32, name="back", tag="turn")
             for chunk in range(CHUNKS):
-                for term, first in ((y_sb[(blk, chunk)], True), (relus[(blk, chunk)], False)):
+                for term, first in ((lines[(blk, chunk)], True), (relus[(blk, chunk)], False)):
                     nc.tensor.matmul(
                         out=back[:, chunk * P : (chunk + 1) * P], lhsT=term[:, j * P : (j + 1) * P],
                         rhs=ident_f32[:], is_transpose=True, start=first, stop=not first,

from contextlib import ExitStack

import concourse.mybir as mybir
from concourse.masks import make_identity

F32 = mybir.dt.float32
BF16 = mybir.dt.bfloat16
U32 = mybir.dt.uint32
U8 = mybir.dt.uint8
FP8X4 = mybir.dt.float8_e4m3fn_x4
ALU = mybir.AluOpType
ACT = mybir.ActivationFunctionType

L, B, D = 512, 8, 512
P = 128
EPS_BN = 1e-5
EPS_LN = 1e-5
TILES = 4
BLOCKS = L * B // (TILES * P)
CHUNKS = D // P
WORDS = D // 2
HELPED = 2
FLOPS = 2 * L * B * D * D


def tile_coattention_pb_t_kernel(tc, x, res_a, ctx_v, W_v, bn_v_g, bn_v_b, prelu_v, ln_g, ln_b, out):
    nc = tc.nc
    with ExitStack() as stack:
        stack.enter_context(tc.manual_schedule())
        const = stack.enter_context(tc.tile_pool(name="const", bufs=1))
        keep = stack.enter_context(tc.tile_pool(name="keep", bufs=1))
        branch = stack.enter_context(tc.tile_pool(name="branch", bufs=2 * CHUNKS))
        scrap = stack.enter_context(tc.tile_pool(name="scrap", bufs=4))
        small = stack.enter_context(tc.tile_pool(name="small", bufs=3))
        gain_psum = stack.enter_context(tc.psum_pool(name="gain_psum", bufs=1))
        y_psum = stack.enter_context(tc.psum_pool(name="y_psum", bufs=3))
        turn_psum = stack.enter_context(tc.psum_pool(name="turn_psum", bufs=4))

        def block_rows(blk):
            group, half = divmod(blk, B // TILES)
            return slice(group * P, (group + 1) * P), slice(half * TILES, (half + 1) * TILES)

        eps_bn = const.tile([P, 1], F32, name="eps_bn")
        nc.vector.memset(eps_bn[:], EPS_BN)
        eps_ln = const.tile([P, 1], F32, name="eps_ln")
        nc.vector.memset(eps_ln[:], EPS_LN)
        warm = const.tile([P, 1], F32, name="warm")
        nc.scalar.activation(out=warm[:], in_=eps_bn[:], func=ACT.Abs_reciprocal_sqrt)

        ones = const.tile([P, P], BF16, name="ones")
        nc.vector.memset(ones[:], 1.0)
        bn_rows = const.tile([P, P], BF16, name="bn_rows")
        nc.vector.memset(bn_rows[:], 0.0)
        ln_rows = const.tile([P, 2, D], BF16, name="ln_rows")
        nc.vector.memset(ln_rows[:], 0.0)
        slope_bf = const.tile([P, 1], BF16, name="slope_bf")
        nc.scalar.dma_start(out=bn_rows[0:CHUNKS, :], in_=bn_v_g.rearrange("(c p) -> c p", p=P))
        nc.scalar.dma_start(out=bn_rows[CHUNKS : 2 * CHUNKS, :], in_=bn_v_b.rearrange("(c p) -> c p", p=P))
        nc.scalar.dma_start(out=ln_rows[0:1, 0, :], in_=ln_g.rearrange("(o d) -> o d", o=1))
        nc.scalar.dma_start(out=ln_rows[0:1, 1, :], in_=ln_b.rearrange("(o d) -> o d", o=1))
        nc.scalar.dma_start(out=slope_bf[:], in_=prelu_v.partition_broadcast(P))
        ident_f32 = const.tile([P, P], F32, name="ident_f32")
        make_identity(nc, ident_f32[:])
        ident_bf = const.tile([P, P], BF16, name="ident_bf")
        make_identity(nc, ident_bf[:])

        with tc.tile_pool(name="ctx", bufs=4) as ctx_pool, tc.tile_pool(name="stage", bufs=3) as stage:
            w_sb = keep.tile([P, CHUNKS * D], BF16, name="w_sb")
            nc.sync.dma_start(
                out=w_sb[:].rearrange("p (c k) -> p c k", c=CHUNKS), in_=W_v.rearrange("(c p) k -> p c k", p=P)
            )
            ctx_sb = []
            for blk in range(BLOCKS):
                l_rows, b_rows = block_rows(blk)
                ctx_t = ctx_pool.tile([P, TILES * D], BF16, name="ctx_t")
                nc.sync.dma_start(
                    out=ctx_t[:].rearrange("p (b k) -> p b k", b=TILES),
                    in_=ctx_v[b_rows, l_rows, :].rearrange("b l k -> l b k"),
                )
                ctx_sb.append(ctx_t)
            x_sb, res_sb = [], []
            for blk in range(BLOCKS):
                l_rows, b_rows = block_rows(blk)
                x_t = keep.tile([P, TILES, D], BF16, name="x_t%d" % blk)
                nc.sync.dma_start(out=x_t[:], in_=x[l_rows, b_rows, :])
                res_t = keep.tile([P, TILES, D], BF16, name="res_t%d" % blk)
                nc.sync.dma_start(out=res_t[:], in_=res_a[b_rows, l_rows, :].rearrange("b l d -> l b d"))
                x_sb.append(x_t)
                res_sb.append(res_t)

            w_codes = keep.tile([P, D], U32, name="w_codes", align_bytes=64)
            w_scales = keep.tile([P, D], U8, name="w_scales", align_bytes=64)
            ctx_codes = keep.tile([P, BLOCKS, TILES * P], U32, name="ctx_codes", align_bytes=64)
            ctx_scales = keep.tile([P, BLOCKS, TILES * P], U8, name="ctx_scales", align_bytes=64)

            def turn_k_onto_partitions(rows_sb):
                words = rows_sb[:].bitcast(F32)
                grouped = stage.tile([P, TILES * P * 4], BF16, name="grouped", align_bytes=64)
                grouped_words = grouped[:].bitcast(F32).rearrange("p (c u) -> p c u", u=2)
                for pair in range(TILES // 2):
                    turned = turn_psum.tile([P, 2, 2 * P], F32, name="turned", tag="turn")
                    for i in range(2):
                        for u in range(2):
                            first = (2 * pair + i) * WORDS + u * P
                            nc.tensor.transpose(
                                out=turned[:, u, i * P : (i + 1) * P], in_=words[:, first : first + P], identity=ident_f32[:]
                            )
                    nc.scalar.copy(
                        out=grouped_words[:, 2 * pair * P : 2 * (pair + 1) * P, :], in_=turned[:].rearrange("p u r -> p r u")
                    )
                return grouped

            def conv_pass(blk, chunk, bank_pool, bank_tag):
                y_t = bank_pool.tile([P, TILES * P], F32, name="y_t", tag=bank_tag)
                c_cols = slice(chunk * P, (chunk + 1) * P)
                nc.tensor.matmul_mx(
                    out=y_t[:],
                    lhsT=w_codes[:, c_cols].bitcast(FP8X4),
                    lhsT_scale=w_scales[:, c_cols],
                    rhs=ctx_codes[:, blk, :].bitcast(FP8X4),
                    rhs_scale=ctx_scales[:, blk, :],
                    start=True,
                    stop=True,
                )
                return y_t

            grouped = {}
            stats = keep.tile([P, CHUNKS, BLOCKS, 6], F32, name="stats")

            def quantise(blk):
                nc.vector.quantize_mx(
                    out=ctx_codes[:, blk, :].bitcast(FP8X4), scales=ctx_scales[:, blk, :], in_=grouped[blk][:]
                )

            def multiply(blk):
                if blk + 2 < BLOCKS:
                    grouped[blk + 2] = turn_k_onto_partitions(ctx_sb[blk + 2])
                if blk + 1 < BLOCKS:
                    quantise(blk + 1)
                for chunk in range(CHUNKS):
                    if chunk % 2 == 0:
                        y_t = conv_pass(blk, chunk, y_psum, "y")
                    else:
                        y_t = conv_pass(blk, chunk, turn_psum, "turn")
                    nc.vector.bn_stats(out=stats[:, chunk, blk, :], in_=y_t[:])

            w_grouped = turn_k_onto_partitions(w_sb)
            grouped[0] = turn_k_onto_partitions(ctx_sb[0])
            nc.vector.quantize_mx(out=w_codes[:].bitcast(FP8X4), scales=w_scales[:], in_=w_grouped[:])
            grouped[1] = turn_k_onto_partitions(ctx_sb[1])
            quantise(0)
            multiply(0)

            bn_turned = turn_psum.tile([P, P], BF16, name="bn_turned", tag="turn")
            nc.tensor.transpose(out=bn_turned[:], in_=bn_rows[:], identity=ident_bf[:])
            bn_cols = const.tile([P, 2 * CHUNKS], F32, name="bn_cols")
            nc.vector.tensor_copy(out=bn_cols[:], in_=bn_turned[:, 0 : 2 * CHUNKS])
            ln_both = gain_psum.tile([P, 2, D], BF16, name="ln_both")
            nc.tensor.matmul(out=ln_both[:, 0, :], lhsT=ones[:], rhs=ln_rows[:, 0, :], start=True, stop=True)
            nc.tensor.matmul(out=ln_both[:, 1, :], lhsT=ones[:], rhs=ln_rows[:, 1, :], start=True, stop=True)
            ln_gain = ln_both[:, 0, :]
            ln_bias = ln_both[:, 1, :]
            slope = const.tile([P, 1], F32, name="slope")
            nc.vector.tensor_copy(out=slope[:], in_=slope_bf[:])
            one_minus_slope = const.tile([P, 1], F32, name="one_minus_slope")
            nc.vector.tensor_scalar(
                out=one_minus_slope[:], in0=slope[:], scalar1=-1.0, scalar2=1.0, op0=ALU.mult, op1=ALU.add
            )
            flip = const.tile([P, 1], F32, name="flip")
            nc.vector.tensor_scalar(out=flip[:], in0=one_minus_slope[:], scalar1=0.0, scalar2=2.0, op0=ALU.is_ge, op1=ALU.mult)
            nc.vector.tensor_scalar_add(out=flip[:], in0=flip[:], scalar1=-1.0)
            line_factor = const.tile([P, 1], F32, name="line_factor")
            nc.vector.tensor_mul(out=line_factor[:], in0=slope[:], in1=flip[:])
            relu_factor = const.tile([P, 1], F32, name="relu_factor")
            nc.vector.tensor_mul(out=relu_factor[:], in0=one_minus_slope[:], in1=flip[:])

            for blk in range(1, BLOCKS):
                multiply(blk)

        sum_pool = stack.enter_context(tc.tile_pool(name="sums", bufs=1))
        sums = []
        for blk in range(BLOCKS):
            sum_t = sum_pool.tile([P, TILES, D], F32, name="sum_t%d" % blk)
            for j in range(TILES):
                nc.gpsimd.tensor_tensor(out=sum_t[:, j, :], in0=x_sb[blk][:, j, :], in1=res_sb[blk][:, j, :], op=ALU.add)
            sums.append(sum_t)

        mean_var = const.tile([P, CHUNKS, 2], F32, name="mean_var")
        for chunk in range(CHUNKS):
            nc.vector.bn_aggr(out=mean_var[:, chunk, :], in_=stats[:, chunk, :, :].rearrange("p b s -> p (b s)"))
        bn_rstd = const.tile([P, CHUNKS], F32, name="bn_rstd")
        nc.scalar.activation(
            out=bn_rstd[:], in_=mean_var[:, :, 1], func=ACT.Abs_reciprocal_sqrt, bias=eps_bn[:], scale=1.0
        )
        bn_scale = const.tile([P, CHUNKS], F32, name="bn_scale")
        nc.vector.tensor_mul(out=bn_scale[:], in0=bn_cols[:, 0:CHUNKS], in1=bn_rstd[:])
        bn_shift = const.tile([P, CHUNKS], F32, name="bn_shift")
        nc.vector.tensor_mul(out=bn_shift[:], in0=mean_var[:, :, 0], in1=bn_scale[:])
        nc.vector.tensor_sub(out=bn_shift[:], in0=bn_cols[:, CHUNKS : 2 * CHUNKS], in1=bn_shift[:])
        line_scale = const.tile([P, CHUNKS], F32, name="line_scale")
        nc.vector.tensor_scalar_mul(out=line_scale[:], in0=bn_scale[:], scalar1=line_factor[:])
        line_shift = const.tile([P, CHUNKS], F32, name="line_shift")
        nc.vector.tensor_scalar_mul(out=line_shift[:], in0=bn_shift[:], scalar1=line_factor[:])
        relu_scale = const.tile([P, CHUNKS], F32, name="relu_scale")
        nc.vector.tensor_scalar_mul(out=relu_scale[:], in0=bn_scale[:], scalar1=relu_factor[:])
        relu_shift = const.tile([P, CHUNKS], F32, name="relu_shift")
        nc.vector.tensor_scalar_mul(out=relu_shift[:], in0=bn_shift[:], scalar1=relu_factor[:])
        neg_relu_shift = const.tile([P, CHUNKS], F32, name="neg_relu_shift")
        nc.vector.tensor_scalar_mul(out=neg_relu_shift[:], in0=relu_shift[:], scalar1=-1.0)
        both_shifts = const.tile([P, CHUNKS], F32, name="both_shifts")
        nc.vector.tensor_add(out=both_shifts[:], in0=line_shift[:], in1=relu_shift[:])

        lines, relus, turned_back, row_sums, neg_means, row_rstds = {}, {}, {}, {}, {}, {}

        def affine(blk, chunk):
            col = slice(chunk, chunk + 1)
            y_t = conv_pass(blk, chunk, y_psum, "y")
            line = branch.tile([P, TILES * P], F32, name="line")
            relu = branch.tile([P, TILES * P], F32, name="relu")
            if blk < HELPED and chunk % 2 == 1:
                nc.vector.tensor_scalar(
                    out=line[:], in0=y_t[:], scalar1=line_scale[:, col], scalar2=both_shifts[:, col],
                    op0=ALU.mult, op1=ALU.add,
                )
                nc.vector.tensor_scalar(
                    out=relu[:], in0=y_t[:], scalar1=relu_scale[:, col], scalar2=neg_relu_shift[:, col],
                    op0=ALU.mult, op1=ALU.max,
                )
            else:
                nc.scalar.activation(
                    out=line[:], in_=y_t[:], func=ACT.Identity, bias=line_shift[:, col], scale=line_scale[:, col]
                )
                nc.scalar.activation(
                    out=relu[:], in_=y_t[:], func=ACT.Relu, bias=relu_shift[:, col], scale=relu_scale[:, col]
                )
            lines[(blk, chunk)] = line
            relus[(blk, chunk)] = relu

        def turn_back(blk, j):
            back = turn_psum.tile([P, D], F32, name="back", tag="turn")
            for chunk in range(CHUNKS):
                for term, first in ((lines[(blk, chunk)], True), (relus[(blk, chunk)], False)):
                    nc.tensor.matmul(
                        out=back[:, chunk * P : (chunk + 1) * P], lhsT=term[:, j * P : (j + 1) * P],
                        rhs=ident_f32[:], is_transpose=True, start=first, stop=not first,
                    )
            turned_back[(blk, j)] = back

        def add_streams(blk, j):
            if j == 0:
                row_sums[blk] = small.tile([P, TILES], F32, name="row_sum")
            nc.vector.scalar_tensor_tensor(
                out=sums[blk][:, j, :], in0=turned_back[(blk, j)][:], scalar=flip[:], in1=sums[blk][:, j, :],
                op0=ALU.mult, op1=ALU.add, accum_out=row_sums[blk][:, j : j + 1],
            )

        def deviation(blk):
            neg_mean = small.tile([P, TILES], F32, name="neg_mean")
            nc.scalar.mul(out=neg_mean[:], in_=row_sums[blk][:], mul=-1.0 / D)
            square_sum = small.tile([P, TILES], F32, name="square_sum")
            for j in range(TILES):
                unread = scrap.tile([P, D], BF16, name="unread")
                nc.scalar.activation(
                    out=unread[:], in_=sums[blk][:, j, :], func=ACT.Square, bias=neg_mean[:, j : j + 1], scale=1.0,
                    accum_out=square_sum[:, j : j + 1],
                )
            row_rstd = small.tile([P, TILES], F32, name="row_rstd")
            nc.scalar.activation(
                out=row_rstd[:], in_=square_sum[:], func=ACT.Abs_reciprocal_sqrt, bias=eps_ln[:], scale=1.0 / D
            )
            neg_means[blk] = neg_mean
            row_rstds[blk] = row_rstd

        def normalise(blk):
            l_rows, b_rows = block_rows(blk)
            first_b = (blk % (B // TILES)) * TILES
            row_rstd = row_rstds[blk]
            for j in range(TILES):
                nc.vector.scalar_tensor_tensor(
                    out=sums[blk][:, j, :], in0=sums[blk][:, j, :], scalar=neg_means[blk][:, j : j + 1], in1=ln_gain,
                    op0=ALU.add, op1=ALU.mult,
                )
            for j in range(TILES):
                nc.vector.scalar_tensor_tensor(
                    out=sums[blk][:, j, :], in0=sums[blk][:, j, :], scalar=row_rstd[:, j : j + 1], in1=ln_bias,
                    op0=ALU.mult, op1=ALU.add,
                )
                nc.sync.dma_start(out=out[l_rows, first_b + j : first_b + j + 1, :], in_=sums[blk][:, j : j + 1, :])

        for step in range(-3, BLOCKS):
            for half in range(2):
                pair = (2 * half, 2 * half + 1)
                if 0 <= step + 3 < BLOCKS:
                    for chunk in pair:
                        affine(step + 3, chunk)
                if half == 0 and 0 <= step + 1 < BLOCKS:
                    for j in range(TILES):
                        add_streams(step + 1, j)
                    deviation(step + 1)
                if 0 <= step + 2 < BLOCKS:
                    for j in pair:
                        turn_back(step + 2, j)
            if 0 <= step:
                normalise(step)
